import numpy as np
import ml_dtypes


def mxq(x, axis, fmt="e4m3"):
    dtype, down = {"e4m3": (ml_dtypes.float8_e4m3fn, 7), "e5m2": (ml_dtypes.float8_e5m2, 14)}[fmt]
    v = np.moveaxis(np.asarray(x, np.float32).astype(ml_dtypes.bfloat16).astype(np.float64), axis, -1)
    blocks = v.reshape(v.shape[:-1] + (-1, 32))
    amax = np.abs(blocks).max(-1, keepdims=True)
    byte = np.maximum(np.where(amax > 0, np.frexp(amax)[1] - 1 + 127, 0) - down, 1)
    scale = np.exp2(byte - 127.0)
    codes = (blocks / scale).astype(np.float32).astype(dtype).astype(np.float64)
    return np.moveaxis((codes * scale).reshape(v.shape), -1, axis)


WIDE = False


def mx_kscale(k):
    if not WIDE:
        return np.ones(k)
    levels = np.array([10, -10, 5, -5, 0])
    a = np.random.permutation(np.resize(levels, k // 512 * 4)).reshape(k // 512, 4)
    idx = np.arange(k)
    return np.exp2(a[idx // 512, idx % 128 // 32])


BF16 = ml_dtypes.bfloat16


def bf(x):
    return np.asarray(x, np.float32).astype(BF16)


def f64(x):
    return np.asarray(x).astype(np.float64)


B, N, C = 8, 1024, 256
Q = N ** 0.25


def setup_inputs():
    s = mx_kscale(N)
    msg = (1.4 * np.random.standard_normal((B, 1, C)) + 1.2 * np.random.standard_normal((B, N, C))) / Q
    return {"A": bf(np.random.uniform(0.0, 1.0, (B, N, N)) * 2.0 / N ** 0.75 * s),
            "msg": bf(msg / s[:, None]),
            "h": bf(np.maximum(np.random.standard_normal((B, N, C)) * 1.35, 0.0)),
            "Ws": bf(np.random.uniform(-1.0, 1.0, (C, C)) * 1.5 / np.sqrt(C)),
            "b": bf(np.random.uniform(-1.0, 1.0, C) * 0.5)}


def reference(A, msg, h, Ws, b):
    agg = mxq(f64(A), 2, "e4m3") @ mxq(f64(msg), 1, "e4m3")
    return np.maximum(agg + f64(h) @ f64(Ws).T + f64(b), 0.0)

@@ -1,0 +1,185 @@
+from contextlib import ExitStack
+
+import concourse.mybir as mybir
+from concourse.masks import make_identity
+
+FLOPS = 2 * 8 * 1024 * 256 * (1024 + 256)
+
+F32 = mybir.dt.float32
+BF16 = mybir.dt.bfloat16
+U32 = mybir.dt.uint32
+U8 = mybir.dt.uint8
+FP8X4 = mybir.dt.float8_e4m3fn_x4
+ADD = mybir.AluOpType.add
+RELU = mybir.ActivationFunctionType.Relu
+P = 128
+PIN = True
+AHEAD = 3
+
+
+def tile_gcnstacking_pb_t_kernel(tc, A, msg, h, Ws, b, out):
+    nc = tc.nc
+    G = 8
+    NQ = 2 * G
+
+    a_view = A.rearrange("g (p q t) k -> g q p (t k)", p=P, q=2, t=4)
+    o_view = out.rearrange("g (p q t) c -> g q p (t c)", p=P, q=2, t=4)
+    h_view = h.rearrange("g (p r) c -> g p (r c)", p=P)
+    m_view = msg.rearrange("g (s p e) c -> g p s (e c)", s=4, p=P, e=2)
+
+    with ExitStack() as ctx:
+        const = ctx.enter_context(tc.tile_pool(name="const", bufs=1))
+        raw = ctx.enter_context(tc.tile_pool(name="raw", bufs=4))
+        work = ctx.enter_context(tc.tile_pool(name="work", bufs=3))
+        psum = ctx.enter_context(tc.psum_pool(name="psum", bufs=1))
+        if PIN:
+            ctx.enter_context(tc.manual_schedule())
+
+        a_raw, h_raw, m_raw = {}, {}, {}
+        a_grp, a_cod, a_scl = {}, {}, {}
+        m_grp, m_cod, m_scl = {}, {}, {}
+        hT, y = {}, {}
+
+        def load_graph(g):
+            a_raw[2 * g] = raw.tile([P, 4096], BF16, name="a_raw", tag="a_raw", bufs=2 * (AHEAD + 1))
+            nc.sync.dma_start(out=a_raw[2 * g][:], in_=a_view[g, 0])
+            m_raw[g] = raw.tile([P, 2048], BF16, name="m_raw", tag="m_raw", bufs=AHEAD + 1)
+            nc.sync.dma_start(out=m_raw[g][:].rearrange("p (s x) -> p s x", s=4), in_=m_view[g])
+            h_raw[g] = raw.tile([P, 2048], BF16, name="h_raw", tag="h_raw", bufs=AHEAD + 1)
+            nc.sync.dma_start(out=h_raw[g][:], in_=h_view[g])
+            a_raw[2 * g + 1] = raw.tile([P, 4096], BF16, name="a_raw", tag="a_raw", bufs=2 * (AHEAD + 1))
+            nc.sync.dma_start(out=a_raw[2 * g + 1][:], in_=a_view[g, 1])
+
+        def transposes(j):
+            g, q = divmod(j, 2)
+            words = a_raw[j][:].bitcast(F32)
+            a_grp[j] = work.tile([P, 4096], BF16, name="a_grp", tag="a_grp", align_bytes=64)
+            grp_words = a_grp[j][:].bitcast(F32)
+            for t in range(4):
+                bank = psum.tile([P, 512], F32, name="at", tag="at", bufs=4)
+                for s in range(4):
+                    lo = 512 * t + 128 * s
+                    nc.tensor.transpose(out=bank[:, 128 * s:128 * (s + 1)], in_=words[:, lo:lo + 128], identity=ident[:])
+                nc.scalar.copy(
+                    out=grp_words[:, 512 * t:512 * (t + 1)].rearrange("p (c i u) -> p c i u", c=2, i=128, u=2),
+                    in_=bank[:].rearrange("p (c u i) -> p c i u", c=2, u=2, i=128),
+                )
+            h_words = h_raw[g][:].bitcast(F32)
+            bank = psum.tile([P, 512], F32, name="ht", tag="ht", bufs=1)
+            for t in range(4):
+                lo = 128 * (4 * q + t)
+                nc.tensor.transpose(out=bank[:, 128 * t:128 * (t + 1)], in_=h_words[:, lo:lo + 128], identity=ident[:])
+            hT[j] = work.tile([P, 512], F32, name="hT", tag="hT")
+            nc.scalar.copy(out=hT[j][:], in_=bank[:])
+
+        def quantise_a(k):
+            a_cod[k] = work.tile([P, 1024], U32, name="a_cod", tag="a_cod", align_bytes=64)
+            a_scl[k] = work.tile([P, 1024], U8, name="a_scl", tag="a_scl", align_bytes=64)
+            nc.vector.quantize_mx(out=a_cod[k][:].bitcast(FP8X4), scales=a_scl[k][:], in_=a_grp[k][:])
+
+        def regroup_msg(g):
+            m_grp[g] = work.tile([P, 2048], BF16, name="m_grp", tag="m_grp", bufs=2, align_bytes=64)
+            for c in range(2):
+                nc.vector.tensor_copy(
+                    out=m_grp[g][:, 1024 * c:1024 * (c + 1)].rearrange("p (n i t) -> p n t i", n=64, i=4, t=4),
+                    in_=m_raw[g][:, 1024 * c:1024 * (c + 1)].rearrange("p (t n i) -> p n t i", t=4, n=64, i=4),
+                )
+
+        def quantise_msg(g):
+            m_cod[g] = work.tile([P, 512], U32, name="m_cod", tag="m_cod", align_bytes=64)
+            m_scl[g] = work.tile([P, 512], U8, name="m_scl", tag="m_scl", align_bytes=64)
+            nc.vector.quantize_mx(out=m_cod[g][:].bitcast(FP8X4), scales=m_scl[g][:], in_=m_grp[g][:])
+
+        def self_term(k):
+            y[k] = work.tile([P, 1024], F32, name="y", tag="y", bufs=6)
+            hT_bf = hT[k][:].bitcast(BF16)
+            for pair in range(2):
+                bank = psum.tile([P, 512], F32, name="acc", tag="acc", bufs=3)
+                for tt in range(2):
+                    t = 2 * pair + tt
+                    for e in range(2):
+                        nc.tensor.matmul(
+                            out=bank[:, 256 * tt:256 * (tt + 1)],
+                            lhsT=hT_bf[:, 256 * t + e:256 * (t + 1):2],
+                            rhs=wsT[:, 256 * e:256 * (e + 1)],
+                            start=(e == 0),
+                            stop=(e == 1),
+                        )
+                nc.vector.tensor_tensor(out=y[k][:, 512 * pair:512 * (pair + 1)], in0=bank[:], in1=bias2[:], op=ADD)
+
+        def aggregate(k):
+            g = k // 2
+            for pair in range(2):
+                bank = psum.tile([P, 512], F32, name="acc", tag="acc", bufs=3)
+                for tt in range(2):
+                    t = 2 * pair + tt
+                    for c in range(2):
+                        lo = 256 * t + 128 * c
+                        nc.tensor.matmul_mx(
+                            out=bank[:, 256 * tt:256 * (tt + 1)],
+                            lhsT=a_cod[k][:, lo:lo + 128].bitcast(FP8X4),
+                            lhsT_scale=a_scl[k][:, lo:lo + 128],
+                            rhs=m_cod[g][:, 256 * c:256 * (c + 1)].bitcast(FP8X4),
+                            rhs_scale=m_scl[g][:, 256 * c:256 * (c + 1)],
+                            start=(c == 0),
+                            stop=(c == 1),
+                        )
+                half = y[k][:, 512 * pair:512 * (pair + 1)]
+                nc.vector.tensor_tensor(out=half, in0=bank[:], in1=half, op=ADD)
+
+        def relu_store(k):
+            g, q = divmod(k, 2)
+            for pair in range(2):
+                half = y[k][:, 512 * pair:512 * (pair + 1)]
+                nc.scalar.activation(out=half, in_=half, func=RELU)
+            nc.sync.dma_start(out=o_view[g, q], in_=y[k][:])
+
+        ident = const.tile([P, P], F32, name="ident")
+        make_identity(nc, ident[:])
+        w_raw = const.tile([P, 512], BF16, name="w_raw")
+        nc.scalar.dma_start(out=w_raw[:].rearrange("p (o c) -> p o c", o=2), in_=Ws.rearrange("(o p) c -> p o c", p=P))
+        b_row = const.tile([P, 256], BF16, name="b_row")
+        nc.vector.memset(b_row[:], 0.0)
+        nc.scalar.dma_start(out=b_row[0:1, :], in_=b.unsqueeze(0))
+        ones = const.tile([P, P], BF16, name="ones")
+        nc.vector.memset(ones[:], 1.0)
+
+        for g in range(AHEAD):
+            load_graph(g)
+
+        wsT = const.tile([P, 512], BF16, name="wsT")
+        bias2 = const.tile([P, 512], F32, name="bias2")
+        w_words = w_raw[:].bitcast(F32)
+        w_bank = psum.tile([P, 512], F32, name="ht", tag="ht", bufs=1)
+        for o in range(2):
+            nc.tensor.transpose(out=w_bank[:, 128 * o:128 * (o + 1)], in_=w_words[:, 128 * o:128 * (o + 1)], identity=ident[:])
+        nc.vector.tensor_copy(
+            out=wsT[:].rearrange("p (e o) -> p e o", e=2),
+            in_=w_bank[:, 0:256].bitcast(BF16).rearrange("p (o e) -> p e o", e=2),
+        )
+        b_bank = psum.tile([P, 512], F32, name="acc", tag="acc", bufs=3)
+        nc.tensor.matmul(out=b_bank[:, 0:256], lhsT=ones[:], rhs=b_row[:], start=True, stop=True)
+        for r in range(2):
+            nc.vector.tensor_copy(out=bias2[:, 256 * r:256 * (r + 1)], in_=b_bank[:, 0:256])
+
+        for j in range(NQ + 2):
+            if j % 2 == 0 and j // 2 + AHEAD < G:
+                load_graph(j // 2 + AHEAD)
+            if j >= 2:
+                relu_store(j - 2)
+            if j < NQ:
+                transposes(j)
+            if j == 0:
+                regroup_msg(0)
+                quantise_msg(0)
+            if 1 <= j <= NQ:
+                k = j - 1
+                quantise_a(k)
+                nxt = k // 2 + 1
+                if nxt < G:
+                    if k % 2 == 0:
+                        regroup_msg(nxt)
+                    else:
+                        quantise_msg(nxt)
+                self_term(k)
+                aggregate(k)

@@ -11,10 +11,12 @@ U32 = mybir.dt.uint32
 U8 = mybir.dt.uint8
 FP8X4 = mybir.dt.float8_e4m3fn_x4
 ADD = mybir.AluOpType.add
+MAX = mybir.AluOpType.max
 RELU = mybir.ActivationFunctionType.Relu
 P = 128
 PIN = True
 AHEAD = 3
+ST_LAG = 3
 
 
 def tile_gcnstacking_pb_t_kernel(tc, A, msg, h, Ws, b, out):
@@ -42,12 +44,18 @@ def tile_gcnstacking_pb_t_kernel(tc, A, msg, h, Ws, b, out):
 
         def load_graph(g):
             a_raw[2 * g] = raw.tile([P, 4096], BF16, name="a_raw", tag="a_raw", bufs=2 * (AHEAD + 1))
-            nc.sync.dma_start(out=a_raw[2 * g][:], in_=a_view[g, 0])
             m_raw[g] = raw.tile([P, 2048], BF16, name="m_raw", tag="m_raw", bufs=AHEAD + 1)
-            nc.sync.dma_start(out=m_raw[g][:].rearrange("p (s x) -> p s x", s=4), in_=m_view[g])
             h_raw[g] = raw.tile([P, 2048], BF16, name="h_raw", tag="h_raw", bufs=AHEAD + 1)
-            nc.sync.dma_start(out=h_raw[g][:], in_=h_view[g])
             a_raw[2 * g + 1] = raw.tile([P, 4096], BF16, name="a_raw", tag="a_raw", bufs=2 * (AHEAD + 1))
+            if g == 0:
+                for t in range(4):
+                    nc.sync.dma_start(out=a_raw[0][:, 1024 * t:1024 * (t + 1)], in_=a_view[0, 0][:, 1024 * t:1024 * (t + 1)])
+                nc.sync.dma_start(out=h_raw[g][:], in_=h_view[g])
+                nc.sync.dma_start(out=m_raw[g][:].rearrange("p (s x) -> p s x", s=4), in_=m_view[g])
+            else:
+                nc.sync.dma_start(out=a_raw[2 * g][:], in_=a_view[g, 0])
+                nc.sync.dma_start(out=m_raw[g][:].rearrange("p (s x) -> p s x", s=4), in_=m_view[g])
+                nc.sync.dma_start(out=h_raw[g][:], in_=h_view[g])
             nc.sync.dma_start(out=a_raw[2 * g + 1][:], in_=a_view[g, 1])
 
         def transposes(j):
@@ -80,10 +88,12 @@ def tile_gcnstacking_pb_t_kernel(tc, A, msg, h, Ws, b, out):
         def regroup_msg(g):
             m_grp[g] = work.tile([P, 2048], BF16, name="m_grp", tag="m_grp", bufs=2, align_bytes=64)
             for c in range(2):
-                nc.vector.tensor_copy(
-                    out=m_grp[g][:, 1024 * c:1024 * (c + 1)].rearrange("p (n i t) -> p n t i", n=64, i=4, t=4),
-                    in_=m_raw[g][:, 1024 * c:1024 * (c + 1)].rearrange("p (t n i) -> p n t i", t=4, n=64, i=4),
-                )
+                dst = m_grp[g][:, 1024 * c:1024 * (c + 1)].rearrange("p (n i t) -> p n t i", n=64, i=4, t=4)
+                src = m_raw[g][:, 1024 * c:1024 * (c + 1)].rearrange("p (t n i) -> p n t i", t=4, n=64, i=4)
+                if g == 0:
+                    nc.vector.tensor_copy(out=dst, in_=src)
+                else:
+                    nc.scalar.copy(out=dst, in_=src)
 
         def quantise_msg(g):
             m_cod[g] = work.tile([P, 512], U32, name="m_cod", tag="m_cod", align_bytes=64)
@@ -91,7 +101,7 @@ def tile_gcnstacking_pb_t_kernel(tc, A, msg, h, Ws, b, out):
             nc.vector.quantize_mx(out=m_cod[g][:].bitcast(FP8X4), scales=m_scl[g][:], in_=m_grp[g][:])
 
         def self_term(k):
-            y[k] = work.tile([P, 1024], F32, name="y", tag="y", bufs=6)
+            y[k] = work.tile([P, 1024], F32, name="y", tag="y", bufs=12)
             hT_bf = hT[k][:].bitcast(BF16)
             for pair in range(2):
                 bank = psum.tile([P, 512], F32, name="acc", tag="acc", bufs=3)
@@ -127,12 +137,18 @@ def tile_gcnstacking_pb_t_kernel(tc, A, msg, h, Ws, b, out):
                 half = y[k][:, 512 * pair:512 * (pair + 1)]
                 nc.vector.tensor_tensor(out=half, in0=bank[:], in1=half, op=ADD)
 
-        def relu_store(k):
-            g, q = divmod(k, 2)
+        def relu(k):
             for pair in range(2):
                 half = y[k][:, 512 * pair:512 * (pair + 1)]
-                nc.scalar.activation(out=half, in_=half, func=RELU)
-            nc.sync.dma_start(out=o_view[g, q], in_=y[k][:])
+                if k == NQ - 1 and pair == 1:
+                    nc.scalar.activation(out=half, in_=half, func=RELU)
+                else:
+                    nc.gpsimd.tensor_scalar(out=half, in0=half, scalar1=0.0, scalar2=0.0, op0=MAX, op1=ADD)
+                if k == NQ - 1:
+                    nc.sync.dma_start(out=o_view[k // 2, k % 2][:, 512 * pair:512 * (pair + 1)], in_=half)
+
+        def store(k):
+            nc.sync.dma_start(out=o_view[k // 2, k % 2], in_=y[k][:])
 
         ident = const.tile([P, P], F32, name="ident")
         make_identity(nc, ident[:])
@@ -144,7 +160,7 @@ def tile_gcnstacking_pb_t_kernel(tc, A, msg, h, Ws, b, out):
         ones = const.tile([P, P], BF16, name="ones")
         nc.vector.memset(ones[:], 1.0)
 
-        for g in range(AHEAD):
+        for g in range(AHEAD + 1):
             load_graph(g)
 
         wsT = const.tile([P, 512], BF16, name="wsT")
@@ -162,24 +178,30 @@ def tile_gcnstacking_pb_t_kernel(tc, A, msg, h, Ws, b, out):
         for r in range(2):
             nc.vector.tensor_copy(out=bias2[:, 256 * r:256 * (r + 1)], in_=b_bank[:, 0:256])
 
-        for j in range(NQ + 2):
+        transposes(0)
+        quantise_a(0)
+        regroup_msg(0)
+        quantise_msg(0)
+        self_term(0)
+        aggregate(0)
+        for j in range(1, NQ + 2):
             if j % 2 == 0 and j // 2 + AHEAD < G:
                 load_graph(j // 2 + AHEAD)
             if j >= 2:
-                relu_store(j - 2)
+                relu(j - 2)
+            if j < NQ and j >= ST_LAG:
+                store(j - ST_LAG)
+            if j == NQ:
+                for k in range(NQ - ST_LAG, NQ - 1):
+                    store(k)
             if j < NQ:
                 transposes(j)
-            if j == 0:
-                regroup_msg(0)
-                quantise_msg(0)
-            if 1 <= j <= NQ:
+            if 2 <= j <= NQ:
                 k = j - 1
                 quantise_a(k)
-                nxt = k // 2 + 1
-                if nxt < G:
-                    if k % 2 == 0:
-                        regroup_msg(nxt)
-                    else:
-                        quantise_msg(nxt)
+                if k % 2 == 1 and k // 2 + 1 < G:
+                    quantise_msg(k // 2 + 1)
                 self_term(k)
                 aggregate(k)
+            if j < NQ and j % 2 == 1 and j // 2 + 1 < G:
+                regroup_msg(j // 2 + 1)

@@ -11,12 +11,13 @@ U32 = mybir.dt.uint32
 U8 = mybir.dt.uint8
 FP8X4 = mybir.dt.float8_e4m3fn_x4
 ADD = mybir.AluOpType.add
-MAX = mybir.AluOpType.max
+MULT = mybir.AluOpType.mult
 RELU = mybir.ActivationFunctionType.Relu
 P = 128
-PIN = True
 AHEAD = 3
 ST_LAG = 3
+WEAVE = True
+V_GRAPHS = 2
 
 
 def tile_gcnstacking_pb_t_kernel(tc, A, msg, h, Ws, b, out):
@@ -34,8 +35,7 @@ def tile_gcnstacking_pb_t_kernel(tc, A, msg, h, Ws, b, out):
         raw = ctx.enter_context(tc.tile_pool(name="raw", bufs=4))
         work = ctx.enter_context(tc.tile_pool(name="work", bufs=3))
         psum = ctx.enter_context(tc.psum_pool(name="psum", bufs=1))
-        if PIN:
-            ctx.enter_context(tc.manual_schedule())
+        ctx.enter_context(tc.manual_schedule())
 
         a_raw, h_raw, m_raw = {}, {}, {}
         a_grp, a_cod, a_scl = {}, {}, {}
@@ -58,56 +58,82 @@ def tile_gcnstacking_pb_t_kernel(tc, A, msg, h, Ws, b, out):
                 nc.sync.dma_start(out=h_raw[g][:], in_=h_view[g])
             nc.sync.dma_start(out=a_raw[2 * g + 1][:], in_=a_view[g, 1])
 
-        def transposes(j):
-            g, q = divmod(j, 2)
+        def a_tile_steps(j, t):
             words = a_raw[j][:].bitcast(F32)
-            a_grp[j] = work.tile([P, 4096], BF16, name="a_grp", tag="a_grp", align_bytes=64)
             grp_words = a_grp[j][:].bitcast(F32)
-            for t in range(4):
-                bank = psum.tile([P, 512], F32, name="at", tag="at", bufs=4)
-                for s in range(4):
-                    lo = 512 * t + 128 * s
-                    nc.tensor.transpose(out=bank[:, 128 * s:128 * (s + 1)], in_=words[:, lo:lo + 128], identity=ident[:])
-                nc.scalar.copy(
-                    out=grp_words[:, 512 * t:512 * (t + 1)].rearrange("p (c i u) -> p c i u", c=2, i=128, u=2),
-                    in_=bank[:].rearrange("p (c u i) -> p c i u", c=2, u=2, i=128),
-                )
+            bank = psum.tile([P, 512], F32, name="at", tag="at", bufs=4)
+
+            def one(s):
+                lo = 512 * t + 128 * s
+                nc.tensor.transpose(out=bank[:, 128 * s:128 * (s + 1)], in_=words[:, lo:lo + 128], identity=ident[:])
+                if s == 3:
+                    nc.scalar.copy(
+                        out=grp_words[:, 512 * t:512 * (t + 1)].rearrange("p (c i u) -> p c i u", c=2, i=128, u=2),
+                        in_=bank[:].rearrange("p (c u i) -> p c i u", c=2, u=2, i=128),
+                    )
+
+            return [(one, s) for s in range(4)]
+
+        def h_steps(j):
+            g, q = divmod(j, 2)
             h_words = h_raw[g][:].bitcast(F32)
             bank = psum.tile([P, 512], F32, name="ht", tag="ht", bufs=1)
-            for t in range(4):
+            hT[j] = work.tile([P, 512], F32, name="hT", tag="hT")
+
+            def one(t):
                 lo = 128 * (4 * q + t)
                 nc.tensor.transpose(out=bank[:, 128 * t:128 * (t + 1)], in_=h_words[:, lo:lo + 128], identity=ident[:])
-            hT[j] = work.tile([P, 512], F32, name="hT", tag="hT")
-            nc.scalar.copy(out=hT[j][:], in_=bank[:])
+                if t == 3:
+                    nc.scalar.copy(out=hT[j][:], in_=bank[:])
+
+            return [(one, t) for t in range(4)]
+
+        def run(steps):
+            for fn, arg in steps:
+                fn(arg)
+
+        def new_group(j):
+            a_grp[j] = work.tile([P, 4096], BF16, name="a_grp", tag="a_grp", align_bytes=64)
 
         def quantise_a(k):
             a_cod[k] = work.tile([P, 1024], U32, name="a_cod", tag="a_cod", align_bytes=64)
             a_scl[k] = work.tile([P, 1024], U8, name="a_scl", tag="a_scl", align_bytes=64)
             nc.vector.quantize_mx(out=a_cod[k][:].bitcast(FP8X4), scales=a_scl[k][:], in_=a_grp[k][:])
 
-        def regroup_msg(g):
-            m_grp[g] = work.tile([P, 2048], BF16, name="m_grp", tag="m_grp", bufs=2, align_bytes=64)
-            for c in range(2):
-                dst = m_grp[g][:, 1024 * c:1024 * (c + 1)].rearrange("p (n i t) -> p n t i", n=64, i=4, t=4)
-                src = m_raw[g][:, 1024 * c:1024 * (c + 1)].rearrange("p (t n i) -> p n t i", t=4, n=64, i=4)
-                if g == 0:
-                    nc.vector.tensor_copy(out=dst, in_=src)
-                else:
-                    nc.scalar.copy(out=dst, in_=src)
+        def regroup_msg(g, c):
+            m_grp[g, c] = work.tile([P, 1024], BF16, name="m_grp%d" % c, tag="m_grp%d" % c, bufs=1, align_bytes=64)
+            if g < V_GRAPHS:
+                nc.vector.tensor_copy(
+                    out=m_grp[g, c][:].rearrange("p (n i t) -> p n t i", n=64, i=4, t=4),
+                    in_=m_raw[g][:, 1024 * c:1024 * (c + 1)].rearrange("p (t n i) -> p n t i", t=4, n=64, i=4),
+                )
+            else:
+                src = m_raw[g][:, 1024 * c:1024 * (c + 1)].rearrange("p (t n) -> p n t", t=4)
+                dst = m_grp[g, c][:].rearrange("p (n t) -> p n t", t=4)
+                for half in range(2):
+                    nc.gpsimd.tensor_scalar(
+                        out=dst[:, 128 * half:128 * (half + 1), :],
+                        in0=src[:, 128 * half:128 * (half + 1), :],
+                        scalar1=1.0, scalar2=0.0, op0=MULT, op1=ADD,
+                    )
 
-        def quantise_msg(g):
-            m_cod[g] = work.tile([P, 512], U32, name="m_cod", tag="m_cod", align_bytes=64)
-            m_scl[g] = work.tile([P, 512], U8, name="m_scl", tag="m_scl", align_bytes=64)
-            nc.vector.quantize_mx(out=m_cod[g][:].bitcast(FP8X4), scales=m_scl[g][:], in_=m_grp[g][:])
+        def quantise_msg(g, c):
+            m_cod[g, c] = work.tile([P, 256], U32, name="m_cod%d" % c, tag="m_cod%d" % c, align_bytes=64)
+            m_scl[g, c] = work.tile([P, 256], U8, name="m_scl%d" % c, tag="m_scl%d" % c, align_bytes=64)
+            nc.vector.quantize_mx(out=m_cod[g, c][:].bitcast(FP8X4), scales=m_scl[g, c][:], in_=m_grp[g, c][:])
 
-        def self_term(k):
+        def self_term(k, woven):
             y[k] = work.tile([P, 1024], F32, name="y", tag="y", bufs=12)
             hT_bf = hT[k][:].bitcast(BF16)
+            n = 0
             for pair in range(2):
                 bank = psum.tile([P, 512], F32, name="acc", tag="acc", bufs=3)
                 for tt in range(2):
                     t = 2 * pair + tt
                     for e in range(2):
+                        if n < len(woven):
+                            run(woven[n:n + 1])
+                        n += 1
                         nc.tensor.matmul(
                             out=bank[:, 256 * tt:256 * (tt + 1)],
                             lhsT=hT_bf[:, 256 * t + e:256 * (t + 1):2],
@@ -129,8 +155,8 @@ def tile_gcnstacking_pb_t_kernel(tc, A, msg, h, Ws, b, out):
                             out=bank[:, 256 * tt:256 * (tt + 1)],
                             lhsT=a_cod[k][:, lo:lo + 128].bitcast(FP8X4),
                             lhsT_scale=a_scl[k][:, lo:lo + 128],
-                            rhs=m_cod[g][:, 256 * c:256 * (c + 1)].bitcast(FP8X4),
-                            rhs_scale=m_scl[g][:, 256 * c:256 * (c + 1)],
+                            rhs=m_cod[g, c][:].bitcast(FP8X4),
+                            rhs_scale=m_scl[g, c][:],
                             start=(c == 0),
                             stop=(c == 1),
                         )
@@ -140,10 +166,7 @@ def tile_gcnstacking_pb_t_kernel(tc, A, msg, h, Ws, b, out):
         def relu(k):
             for pair in range(2):
                 half = y[k][:, 512 * pair:512 * (pair + 1)]
-                if k == NQ - 1 and pair == 1:
-                    nc.scalar.activation(out=half, in_=half, func=RELU)
-                else:
-                    nc.gpsimd.tensor_scalar(out=half, in0=half, scalar1=0.0, scalar2=0.0, op0=MAX, op1=ADD)
+                nc.scalar.activation(out=half, in_=half, func=RELU)
                 if k == NQ - 1:
                     nc.sync.dma_start(out=o_view[k // 2, k % 2][:, 512 * pair:512 * (pair + 1)], in_=half)
 
@@ -178,30 +201,44 @@ def tile_gcnstacking_pb_t_kernel(tc, A, msg, h, Ws, b, out):
         for r in range(2):
             nc.vector.tensor_copy(out=bias2[:, 256 * r:256 * (r + 1)], in_=b_bank[:, 0:256])
 
-        transposes(0)
-        quantise_a(0)
-        regroup_msg(0)
-        quantise_msg(0)
-        self_term(0)
-        aggregate(0)
-        for j in range(1, NQ + 2):
-            if j % 2 == 0 and j // 2 + AHEAD < G:
+        for j in range(NQ + 2):
+            k = j - 1
+            if j >= 2 and j % 2 == 0 and j // 2 + AHEAD < G:
                 load_graph(j // 2 + AHEAD)
             if j >= 2:
                 relu(j - 2)
-            if j < NQ and j >= ST_LAG:
+            if ST_LAG <= j < NQ:
                 store(j - ST_LAG)
             if j == NQ:
-                for k in range(NQ - ST_LAG, NQ - 1):
-                    store(k)
+                for kk in range(NQ - ST_LAG, NQ - 1):
+                    store(kk)
+            woven = []
             if j < NQ:
-                transposes(j)
+                new_group(j)
+                bunched = 3 if (WEAVE and j >= 2) else 4
+                for t in range(bunched):
+                    run(a_tile_steps(j, t))
+                if bunched == 3:
+                    woven = a_tile_steps(j, 3) + h_steps(j)
+                else:
+                    run(h_steps(j))
+            if j == 0:
+                quantise_a(0)
+                regroup_msg(0, 0)
+                regroup_msg(0, 1)
+                quantise_msg(0, 0)
+                quantise_msg(0, 1)
+                self_term(0, [])
+                aggregate(0)
             if 2 <= j <= NQ:
-                k = j - 1
                 quantise_a(k)
-                if k % 2 == 1 and k // 2 + 1 < G:
-                    quantise_msg(k // 2 + 1)
-                self_term(k)
+                if k == 1:
+                    regroup_msg(1, 0)
+                    regroup_msg(1, 1)
+                g, c = divmod(k + 1, 2)
+                if g < G:
+                    quantise_msg(g, c)
+                    if V_GRAPHS <= g + 1 < G:
+                        regroup_msg(g + 1, c)
+                self_term(k, woven)
                 aggregate(k)
-            if j < NQ and j % 2 == 1 and j // 2 + 1 < G:
-                regroup_msg(j // 2 + 1)

@@ -18,6 +18,7 @@ AHEAD = 3
 ST_LAG = 3
 WEAVE = True
 V_GRAPHS = 2
+WHOLE_A = (2, 3, 4, 5, 6)
 
 
 def tile_gcnstacking_pb_t_kernel(tc, A, msg, h, Ws, b, out):
@@ -25,8 +26,8 @@ def tile_gcnstacking_pb_t_kernel(tc, A, msg, h, Ws, b, out):
     G = 8
     NQ = 2 * G
 
-    a_view = A.rearrange("g (p q t) k -> g q p (t k)", p=P, q=2, t=4)
-    o_view = out.rearrange("g (p q t) c -> g q p (t c)", p=P, q=2, t=4)
+    a_view = A.rearrange("g (p r) k -> g p (r k)", p=P)
+    o_view = out.rearrange("g (p r) c -> g p (r c)", p=P)
     h_view = h.rearrange("g (p r) c -> g p (r c)", p=P)
     m_view = msg.rearrange("g (s p e) c -> g p s (e c)", s=4, p=P, e=2)
 
@@ -40,31 +41,38 @@ def tile_gcnstacking_pb_t_kernel(tc, A, msg, h, Ws, b, out):
         a_raw, h_raw, m_raw = {}, {}, {}
         a_grp, a_cod, a_scl = {}, {}, {}
         m_grp, m_cod, m_scl = {}, {}, {}
-        hT, y = {}, {}
+        hT, y, y_graph = {}, {}, {}
+
+        def load_a(g, lo, hi):
+            nc.sync.dma_start(out=a_raw[g][:, 1024 * lo:1024 * hi], in_=a_view[g][:, 1024 * lo:1024 * hi])
 
         def load_graph(g):
-            a_raw[2 * g] = raw.tile([P, 4096], BF16, name="a_raw", tag="a_raw", bufs=2 * (AHEAD + 1))
+            a_raw[g] = raw.tile([P, 8192], BF16, name="a_raw", tag="a_raw", bufs=AHEAD + 1)
             m_raw[g] = raw.tile([P, 2048], BF16, name="m_raw", tag="m_raw", bufs=AHEAD + 1)
             h_raw[g] = raw.tile([P, 2048], BF16, name="h_raw", tag="h_raw", bufs=AHEAD + 1)
-            a_raw[2 * g + 1] = raw.tile([P, 4096], BF16, name="a_raw", tag="a_raw", bufs=2 * (AHEAD + 1))
             if g == 0:
                 for t in range(4):
-                    nc.sync.dma_start(out=a_raw[0][:, 1024 * t:1024 * (t + 1)], in_=a_view[0, 0][:, 1024 * t:1024 * (t + 1)])
+                    load_a(g, t, t + 1)
                 nc.sync.dma_start(out=h_raw[g][:], in_=h_view[g])
                 nc.sync.dma_start(out=m_raw[g][:].rearrange("p (s x) -> p s x", s=4), in_=m_view[g])
+                load_a(g, 4, 8)
+            elif g in WHOLE_A:
+                load_a(g, 0, 8)
+                nc.sync.dma_start(out=m_raw[g][:].rearrange("p (s x) -> p s x", s=4), in_=m_view[g])
+                nc.sync.dma_start(out=h_raw[g][:], in_=h_view[g])
             else:
-                nc.sync.dma_start(out=a_raw[2 * g][:], in_=a_view[g, 0])
+                load_a(g, 0, 4)
                 nc.sync.dma_start(out=m_raw[g][:].rearrange("p (s x) -> p s x", s=4), in_=m_view[g])
                 nc.sync.dma_start(out=h_raw[g][:], in_=h_view[g])
-            nc.sync.dma_start(out=a_raw[2 * g + 1][:], in_=a_view[g, 1])
+                load_a(g, 4, 8)
 
         def a_tile_steps(j, t):
-            words = a_raw[j][:].bitcast(F32)
+            words = a_raw[j // 2][:].bitcast(F32)
             grp_words = a_grp[j][:].bitcast(F32)
             bank = psum.tile([P, 512], F32, name="at", tag="at", bufs=4)
 
             def one(s):
-                lo = 512 * t + 128 * s
+                lo = 2048 * (j % 2) + 512 * t + 128 * s
                 nc.tensor.transpose(out=bank[:, 128 * s:128 * (s + 1)], in_=words[:, lo:lo + 128], identity=ident[:])
                 if s == 3:
                     nc.scalar.copy(
@@ -123,7 +131,9 @@ def tile_gcnstacking_pb_t_kernel(tc, A, msg, h, Ws, b, out):
             nc.vector.quantize_mx(out=m_cod[g, c][:].bitcast(FP8X4), scales=m_scl[g, c][:], in_=m_grp[g, c][:])
 
         def self_term(k, woven):
-            y[k] = work.tile([P, 1024], F32, name="y", tag="y", bufs=12)
+            if k % 2 == 0:
+                y_graph[k // 2] = work.tile([P, 2048], F32, name="y", tag="y", bufs=6)
+            y[k] = y_graph[k // 2][:, 1024 * (k % 2):1024 * (k % 2 + 1)]
             hT_bf = hT[k][:].bitcast(BF16)
             n = 0
             for pair in range(2):
@@ -168,10 +178,15 @@ def tile_gcnstacking_pb_t_kernel(tc, A, msg, h, Ws, b, out):
                 half = y[k][:, 512 * pair:512 * (pair + 1)]
                 nc.scalar.activation(out=half, in_=half, func=RELU)
                 if k == NQ - 1:
-                    nc.sync.dma_start(out=o_view[k // 2, k % 2][:, 512 * pair:512 * (pair + 1)], in_=half)
+                    lo = 1024 * (k % 2) + 512 * pair
+                    nc.sync.dma_start(out=o_view[k // 2][:, lo:lo + 512], in_=half)
 
         def store(k):
-            nc.sync.dma_start(out=o_view[k // 2, k % 2], in_=y[k][:])
+            g, q = divmod(k, 2)
+            if g == G - 1:
+                nc.sync.dma_start(out=o_view[g][:, 1024 * q:1024 * (q + 1)], in_=y[k])
+            elif q == 1:
+                nc.sync.dma_start(out=o_view[g], in_=y_graph[g][:])
 
         ident = const.tile([P, P], F32, name="ident")
         make_identity(nc, ident[:])

@@ -15,10 +15,9 @@ MULT = mybir.AluOpType.mult
 RELU = mybir.ActivationFunctionType.Relu
 P = 128
 AHEAD = 3
-ST_LAG = 3
+ST_LAG = 4
 WEAVE = True
 V_GRAPHS = 2
-WHOLE_A = (2, 3, 4, 5, 6)
 
 
 def tile_gcnstacking_pb_t_kernel(tc, A, msg, h, Ws, b, out):
@@ -26,8 +25,8 @@ def tile_gcnstacking_pb_t_kernel(tc, A, msg, h, Ws, b, out):
     G = 8
     NQ = 2 * G
 
-    a_view = A.rearrange("g (p r) k -> g p (r k)", p=P)
-    o_view = out.rearrange("g (p r) c -> g p (r c)", p=P)
+    a_view = A.rearrange("g (p q t) k -> g q p (t k)", p=P, q=2, t=4)
+    o_view = out.rearrange("g (p q t) c -> g q p (t c)", p=P, q=2, t=4)
     h_view = h.rearrange("g (p r) c -> g p (r c)", p=P)
     m_view = msg.rearrange("g (s p e) c -> g p s (e c)", s=4, p=P, e=2)
 
@@ -41,38 +40,39 @@ def tile_gcnstacking_pb_t_kernel(tc, A, msg, h, Ws, b, out):
         a_raw, h_raw, m_raw = {}, {}, {}
         a_grp, a_cod, a_scl = {}, {}, {}
         m_grp, m_cod, m_scl = {}, {}, {}
-        hT, y, y_graph = {}, {}, {}
+        hT, y = {}, {}
 
-        def load_a(g, lo, hi):
-            nc.sync.dma_start(out=a_raw[g][:, 1024 * lo:1024 * hi], in_=a_view[g][:, 1024 * lo:1024 * hi])
+        def load_msg(g):
+            m_raw[g] = raw.tile([P, 2048], BF16, name="m_raw", tag="m_raw", bufs=AHEAD + 2)
+            nc.sync.dma_start(out=m_raw[g][:].rearrange("p (s x) -> p s x", s=4), in_=m_view[g])
 
         def load_graph(g):
-            a_raw[g] = raw.tile([P, 8192], BF16, name="a_raw", tag="a_raw", bufs=AHEAD + 1)
-            m_raw[g] = raw.tile([P, 2048], BF16, name="m_raw", tag="m_raw", bufs=AHEAD + 1)
+            a_raw[2 * g] = raw.tile([P, 4096], BF16, name="a_raw", tag="a_raw", bufs=2 * (AHEAD + 1))
             h_raw[g] = raw.tile([P, 2048], BF16, name="h_raw", tag="h_raw", bufs=AHEAD + 1)
+            a_raw[2 * g + 1] = raw.tile([P, 4096], BF16, name="a_raw", tag="a_raw", bufs=2 * (AHEAD + 1))
             if g == 0:
                 for t in range(4):
-                    load_a(g, t, t + 1)
+                    nc.sync.dma_start(out=a_raw[0][:, 1024 * t:1024 * (t + 1)], in_=a_view[0, 0][:, 1024 * t:1024 * (t + 1)])
                 nc.sync.dma_start(out=h_raw[g][:], in_=h_view[g])
-                nc.sync.dma_start(out=m_raw[g][:].rearrange("p (s x) -> p s x", s=4), in_=m_view[g])
-                load_a(g, 4, 8)
-            elif g in WHOLE_A:
-                load_a(g, 0, 8)
-                nc.sync.dma_start(out=m_raw[g][:].rearrange("p (s x) -> p s x", s=4), in_=m_view[g])
-                nc.sync.dma_start(out=h_raw[g][:], in_=h_view[g])
+                load_msg(0)
             else:
-                load_a(g, 0, 4)
-                nc.sync.dma_start(out=m_raw[g][:].rearrange("p (s x) -> p s x", s=4), in_=m_view[g])
+                if g == 2:
+                    load_msg(2)
+                nc.sync.dma_start(out=a_raw[2 * g][:], in_=a_view[g, 0])
+                if g == 1:
+                    load_msg(1)
+                elif g + 1 < G:
+                    load_msg(g + 1)
                 nc.sync.dma_start(out=h_raw[g][:], in_=h_view[g])
-                load_a(g, 4, 8)
+            nc.sync.dma_start(out=a_raw[2 * g + 1][:], in_=a_view[g, 1])
 
         def a_tile_steps(j, t):
-            words = a_raw[j // 2][:].bitcast(F32)
+            words = a_raw[j][:].bitcast(F32)
             grp_words = a_grp[j][:].bitcast(F32)
             bank = psum.tile([P, 512], F32, name="at", tag="at", bufs=4)
 
             def one(s):
-                lo = 2048 * (j % 2) + 512 * t + 128 * s
+                lo = 512 * t + 128 * s
                 nc.tensor.transpose(out=bank[:, 128 * s:128 * (s + 1)], in_=words[:, lo:lo + 128], identity=ident[:])
                 if s == 3:
                     nc.scalar.copy(
@@ -118,12 +118,7 @@ def tile_gcnstacking_pb_t_kernel(tc, A, msg, h, Ws, b, out):
             else:
                 src = m_raw[g][:, 1024 * c:1024 * (c + 1)].rearrange("p (t n) -> p n t", t=4)
                 dst = m_grp[g, c][:].rearrange("p (n t) -> p n t", t=4)
-                for half in range(2):
-                    nc.gpsimd.tensor_scalar(
-                        out=dst[:, 128 * half:128 * (half + 1), :],
-                        in0=src[:, 128 * half:128 * (half + 1), :],
-                        scalar1=1.0, scalar2=0.0, op0=MULT, op1=ADD,
-                    )
+                nc.gpsimd.tensor_scalar(out=dst, in0=src, scalar1=1.0, scalar2=0.0, op0=MULT, op1=ADD)
 
         def quantise_msg(g, c):
             m_cod[g, c] = work.tile([P, 256], U32, name="m_cod%d" % c, tag="m_cod%d" % c, align_bytes=64)
@@ -131,9 +126,7 @@ def tile_gcnstacking_pb_t_kernel(tc, A, msg, h, Ws, b, out):
             nc.vector.quantize_mx(out=m_cod[g, c][:].bitcast(FP8X4), scales=m_scl[g, c][:], in_=m_grp[g, c][:])
 
         def self_term(k, woven):
-            if k % 2 == 0:
-                y_graph[k // 2] = work.tile([P, 2048], F32, name="y", tag="y", bufs=6)
-            y[k] = y_graph[k // 2][:, 1024 * (k % 2):1024 * (k % 2 + 1)]
+            y[k] = work.tile([P, 1024], F32, name="y", tag="y", bufs=12)
             hT_bf = hT[k][:].bitcast(BF16)
             n = 0
             for pair in range(2):
@@ -178,15 +171,10 @@ def tile_gcnstacking_pb_t_kernel(tc, A, msg, h, Ws, b, out):
                 half = y[k][:, 512 * pair:512 * (pair + 1)]
                 nc.scalar.activation(out=half, in_=half, func=RELU)
                 if k == NQ - 1:
-                    lo = 1024 * (k % 2) + 512 * pair
-                    nc.sync.dma_start(out=o_view[k // 2][:, lo:lo + 512], in_=half)
+                    nc.sync.dma_start(out=o_view[k // 2, k % 2][:, 512 * pair:512 * (pair + 1)], in_=half)
 
         def store(k):
-            g, q = divmod(k, 2)
-            if g == G - 1:
-                nc.sync.dma_start(out=o_view[g][:, 1024 * q:1024 * (q + 1)], in_=y[k])
-            elif q == 1:
-                nc.sync.dma_start(out=o_view[g], in_=y_graph[g][:])
+            nc.sync.dma_start(out=o_view[k // 2, k % 2], in_=y[k][:])
 
         ident = const.tile([P, P], F32, name="ident")
         make_identity(nc, ident[:])
@@ -216,17 +204,18 @@ def tile_gcnstacking_pb_t_kernel(tc, A, msg, h, Ws, b, out):
         for r in range(2):
             nc.vector.tensor_copy(out=bias2[:, 256 * r:256 * (r + 1)], in_=b_bank[:, 0:256])
 
+        def stores_by(j):
+            lag = ST_LAG if j <= 2 * (G - 1 - AHEAD) else 2
+            return max(0, min(j - lag + 1, NQ - 1))
+
         for j in range(NQ + 2):
             k = j - 1
             if j >= 2 and j % 2 == 0 and j // 2 + AHEAD < G:
                 load_graph(j // 2 + AHEAD)
             if j >= 2:
                 relu(j - 2)
-            if ST_LAG <= j < NQ:
-                store(j - ST_LAG)
-            if j == NQ:
-                for kk in range(NQ - ST_LAG, NQ - 1):
-                    store(kk)
+            for kk in range(stores_by(j - 1), stores_by(j)):
+                store(kk)
             woven = []
             if j < NQ:
                 new_group(j)

@@ -18,15 +18,23 @@ AHEAD = 3
 ST_LAG = 4
 WEAVE = True
 V_GRAPHS = 2
+HEAD = (2, 2, 4)
+TAIL = (4, 2, 2)
 
 
 def tile_gcnstacking_pb_t_kernel(tc, A, msg, h, Ws, b, out):
     nc = tc.nc
     G = 8
-    NQ = 2 * G
+    rounds = []
+    for g in range(G):
+        r0 = 0
+        for n in (HEAD if g == 0 else (TAIL if g == G - 1 else (4, 4))):
+            rounds.append((g, r0, n))
+            r0 += n
+    NR = len(rounds)
 
     a_view = A.rearrange("g (p q t) k -> g q p (t k)", p=P, q=2, t=4)
-    o_view = out.rearrange("g (p q t) c -> g q p (t c)", p=P, q=2, t=4)
+    o_view = out.rearrange("g (p r) c -> g p (r c)", p=P)
     h_view = h.rearrange("g (p r) c -> g p (r c)", p=P)
     m_view = msg.rearrange("g (s p e) c -> g p s (e c)", s=4, p=P, e=2)
 
@@ -67,12 +75,14 @@ def tile_gcnstacking_pb_t_kernel(tc, A, msg, h, Ws, b, out):
             nc.sync.dma_start(out=a_raw[2 * g + 1][:], in_=a_view[g, 1])
 
         def a_tile_steps(j, t):
-            words = a_raw[j][:].bitcast(F32)
+            g, r0, n = rounds[j]
+            r = r0 + t
+            words = a_raw[2 * g + r // 4][:].bitcast(F32)
             grp_words = a_grp[j][:].bitcast(F32)
             bank = psum.tile([P, 512], F32, name="at", tag="at", bufs=4)
 
             def one(s):
-                lo = 512 * t + 128 * s
+                lo = 512 * (r % 4) + 128 * s
                 nc.tensor.transpose(out=bank[:, 128 * s:128 * (s + 1)], in_=words[:, lo:lo + 128], identity=ident[:])
                 if s == 3:
                     nc.scalar.copy(
@@ -83,18 +93,18 @@ def tile_gcnstacking_pb_t_kernel(tc, A, msg, h, Ws, b, out):
             return [(one, s) for s in range(4)]
 
         def h_steps(j):
-            g, q = divmod(j, 2)
+            g, r0, n = rounds[j]
             h_words = h_raw[g][:].bitcast(F32)
             bank = psum.tile([P, 512], F32, name="ht", tag="ht", bufs=1)
             hT[j] = work.tile([P, 512], F32, name="hT", tag="hT")
 
             def one(t):
-                lo = 128 * (4 * q + t)
+                lo = 128 * (r0 + t)
                 nc.tensor.transpose(out=bank[:, 128 * t:128 * (t + 1)], in_=h_words[:, lo:lo + 128], identity=ident[:])
-                if t == 3:
-                    nc.scalar.copy(out=hT[j][:], in_=bank[:])
+                if t == n - 1:
+                    nc.scalar.copy(out=hT[j][:, 0:128 * n], in_=bank[:, 0:128 * n])
 
-            return [(one, t) for t in range(4)]
+            return [(one, t) for t in range(n)]
 
         def run(steps):
             for fn, arg in steps:
@@ -106,7 +116,10 @@ def tile_gcnstacking_pb_t_kernel(tc, A, msg, h, Ws, b, out):
         def quantise_a(k):
             a_cod[k] = work.tile([P, 1024], U32, name="a_cod", tag="a_cod", align_bytes=64)
             a_scl[k] = work.tile([P, 1024], U8, name="a_scl", tag="a_scl", align_bytes=64)
-            nc.vector.quantize_mx(out=a_cod[k][:].bitcast(FP8X4), scales=a_scl[k][:], in_=a_grp[k][:])
+            n = rounds[k][2]
+            nc.vector.quantize_mx(
+                out=a_cod[k][:, 0:256 * n].bitcast(FP8X4), scales=a_scl[k][:, 0:256 * n], in_=a_grp[k][:, 0:1024 * n]
+            )
 
         def regroup_msg(g, c):
             m_grp[g, c] = work.tile([P, 1024], BF16, name="m_grp%d" % c, tag="m_grp%d" % c, bufs=1, align_bytes=64)
@@ -128,15 +141,14 @@ def tile_gcnstacking_pb_t_kernel(tc, A, msg, h, Ws, b, out):
         def self_term(k, woven):
             y[k] = work.tile([P, 1024], F32, name="y", tag="y", bufs=12)
             hT_bf = hT[k][:].bitcast(BF16)
-            n = 0
-            for pair in range(2):
+            m = 0
+            for pair in range(rounds[k][2] // 2):
                 bank = psum.tile([P, 512], F32, name="acc", tag="acc", bufs=3)
                 for tt in range(2):
                     t = 2 * pair + tt
                     for e in range(2):
-                        if n < len(woven):
-                            run(woven[n:n + 1])
-                        n += 1
+                        run(woven[m:m + 1])
+                        m += 1
                         nc.tensor.matmul(
                             out=bank[:, 256 * tt:256 * (tt + 1)],
                             lhsT=hT_bf[:, 256 * t + e:256 * (t + 1):2],
@@ -147,8 +159,8 @@ def tile_gcnstacking_pb_t_kernel(tc, A, msg, h, Ws, b, out):
                 nc.vector.tensor_tensor(out=y[k][:, 512 * pair:512 * (pair + 1)], in0=bank[:], in1=bias2[:], op=ADD)
 
         def aggregate(k):
-            g = k // 2
-            for pair in range(2):
+            g = rounds[k][0]
+            for pair in range(rounds[k][2] // 2):
                 bank = psum.tile([P, 512], F32, name="acc", tag="acc", bufs=3)
                 for tt in range(2):
                     t = 2 * pair + tt
@@ -167,14 +179,17 @@ def tile_gcnstacking_pb_t_kernel(tc, A, msg, h, Ws, b, out):
                 nc.vector.tensor_tensor(out=half, in0=bank[:], in1=half, op=ADD)
 
         def relu(k):
-            for pair in range(2):
+            g, r0, n = rounds[k]
+            for pair in range(n // 2):
                 half = y[k][:, 512 * pair:512 * (pair + 1)]
                 nc.scalar.activation(out=half, in_=half, func=RELU)
-                if k == NQ - 1:
-                    nc.sync.dma_start(out=o_view[k // 2, k % 2][:, 512 * pair:512 * (pair + 1)], in_=half)
+                if k == NR - 1:
+                    lo = 256 * r0 + 512 * pair
+                    nc.sync.dma_start(out=o_view[g][:, lo:lo + 512], in_=half)
 
         def store(k):
-            nc.sync.dma_start(out=o_view[k // 2, k % 2], in_=y[k][:])
+            g, r0, n = rounds[k]
+            nc.sync.dma_start(out=o_view[g][:, 256 * r0:256 * (r0 + n)], in_=y[k][:, 0:256 * n])
 
         ident = const.tile([P, P], F32, name="ident")
         make_identity(nc, ident[:])
@@ -205,27 +220,27 @@ def tile_gcnstacking_pb_t_kernel(tc, A, msg, h, Ws, b, out):
             nc.vector.tensor_copy(out=bias2[:, 256 * r:256 * (r + 1)], in_=b_bank[:, 0:256])
 
         def stores_by(j):
-            lag = ST_LAG if j <= 2 * (G - 1 - AHEAD) else 2
-            return max(0, min(j - lag + 1, NQ - 1))
+            lag = ST_LAG if j <= rounds.index((G - 1 - AHEAD, 0, 4)) else 2
+            return max(0, min(j - lag + 1, NR - 1))
 
-        for j in range(NQ + 2):
+        for j in range(NR + 2):
             k = j - 1
-            if j >= 2 and j % 2 == 0 and j // 2 + AHEAD < G:
-                load_graph(j // 2 + AHEAD)
+            if 1 <= j < NR and rounds[j][1] == 0 and rounds[j][0] + AHEAD < G:
+                load_graph(rounds[j][0] + AHEAD)
             if j >= 2:
                 relu(j - 2)
             for kk in range(stores_by(j - 1), stores_by(j)):
                 store(kk)
             woven = []
-            if j < NQ:
+            if j < NR:
                 new_group(j)
-                bunched = 3 if (WEAVE and j >= 2) else 4
-                for t in range(bunched):
-                    run(a_tile_steps(j, t))
-                if bunched == 3:
-                    woven = a_tile_steps(j, 3) + h_steps(j)
-                else:
-                    run(h_steps(j))
+                steps = []
+                for t in range(rounds[j][2]):
+                    steps.extend(a_tile_steps(j, t))
+                steps.extend(h_steps(j))
+                w = min(2 * rounds[k][2], 4 + rounds[j][2]) if (WEAVE and j >= 2) else 0
+                run(steps[:len(steps) - w])
+                woven = steps[len(steps) - w:]
             if j == 0:
                 quantise_a(0)
                 regroup_msg(0, 0)
@@ -234,15 +249,19 @@ def tile_gcnstacking_pb_t_kernel(tc, A, msg, h, Ws, b, out):
                 quantise_msg(0, 1)
                 self_term(0, [])
                 aggregate(0)
-            if 2 <= j <= NQ:
+            if 2 <= j <= NR:
+                g, r0, n = rounds[k]
                 quantise_a(k)
-                if k == 1:
-                    regroup_msg(1, 0)
-                    regroup_msg(1, 1)
-                g, c = divmod(k + 1, 2)
-                if g < G:
-                    quantise_msg(g, c)
+                if r0 + n == 8 and g + 1 < G:
+                    if g + 1 < V_GRAPHS:
+                        regroup_msg(g + 1, 0)
+                        regroup_msg(g + 1, 1)
+                    quantise_msg(g + 1, 0)
+                    if V_GRAPHS <= g + 2 < G:
+                        regroup_msg(g + 2, 0)
+                if r0 == 0 and g >= 1:
+                    quantise_msg(g, 1)
                     if V_GRAPHS <= g + 1 < G:
-                        regroup_msg(g + 1, c)
+                        regroup_msg(g + 1, 1)
                 self_term(k, woven)
                 aggregate(k)

from contextlib import ExitStack

import concourse.mybir as mybir
from concourse.masks import make_identity

FLOPS = 2 * 8 * 1024 * 256 * (1024 + 256)

F32 = mybir.dt.float32
BF16 = mybir.dt.bfloat16
U32 = mybir.dt.uint32
U8 = mybir.dt.uint8
FP8X4 = mybir.dt.float8_e4m3fn_x4
ADD = mybir.AluOpType.add
MULT = mybir.AluOpType.mult
RELU = mybir.ActivationFunctionType.Relu
P = 128
AHEAD = 3
ST_LAG = 4
WEAVE = True
V_GRAPHS = 2
HEAD = (2, 2, 4)
TAIL = (4, 2, 2)


def tile_gcnstacking_pb_t_kernel(tc, A, msg, h, Ws, b, out):
    nc = tc.nc
    G = 8
    rounds = []
    for g in range(G):
        r0 = 0
        for n in (HEAD if g == 0 else (TAIL if g == G - 1 else (4, 4))):
            rounds.append((g, r0, n))
            r0 += n
    NR = len(rounds)

    a_view = A.rearrange("g (p q t) k -> g q p (t k)", p=P, q=2, t=4)
    o_view = out.rearrange("g (p r) c -> g p (r c)", p=P)
    h_view = h.rearrange("g (p r) c -> g p (r c)", p=P)
    m_view = msg.rearrange("g (s p e) c -> g p s (e c)", s=4, p=P, e=2)

    with ExitStack() as ctx:
        const = ctx.enter_context(tc.tile_pool(name="const", bufs=1))
        raw = ctx.enter_context(tc.tile_pool(name="raw", bufs=4))
        work = ctx.enter_context(tc.tile_pool(name="work", bufs=3))
        psum = ctx.enter_context(tc.psum_pool(name="psum", bufs=1))
        ctx.enter_context(tc.manual_schedule())

        a_raw, h_raw, m_raw = {}, {}, {}
        a_grp, a_cod, a_scl = {}, {}, {}
        m_grp, m_cod, m_scl = {}, {}, {}
        hT, y = {}, {}

        def load_msg(g):
            m_raw[g] = raw.tile([P, 2048], BF16, name="m_raw", tag="m_raw", bufs=AHEAD + 2)
            nc.sync.dma_start(out=m_raw[g][:].rearrange("p (s x) -> p s x", s=4), in_=m_view[g])

        def load_graph(g):
            a_raw[2 * g] = raw.tile([P, 4096], BF16, name="a_raw", tag="a_raw", bufs=2 * (AHEAD + 1))
            h_raw[g] = raw.tile([P, 2048], BF16, name="h_raw", tag="h_raw", bufs=AHEAD + 1)
            a_raw[2 * g + 1] = raw.tile([P, 4096], BF16, name="a_raw", tag="a_raw", bufs=2 * (AHEAD + 1))
            if g == 0:
                for t in range(4):
                    nc.sync.dma_start(out=a_raw[0][:, 1024 * t:1024 * (t + 1)], in_=a_view[0, 0][:, 1024 * t:1024 * (t + 1)])
                nc.sync.dma_start(out=h_raw[g][:], in_=h_view[g])
                load_msg(0)
            else:
                if g == 2:
                    load_msg(2)
                nc.sync.dma_start(out=a_raw[2 * g][:], in_=a_view[g, 0])
                if g == 1:
                    load_msg(1)
                elif g + 1 < G:
                    load_msg(g + 1)
                nc.sync.dma_start(out=h_raw[g][:], in_=h_view[g])
            nc.sync.dma_start(out=a_raw[2 * g + 1][:], in_=a_view[g, 1])

        def a_tile_steps(j, t):
            g, r0, n = rounds[j]
            r = r0 + t
            words = a_raw[2 * g + r // 4][:].bitcast(F32)
            grp_words = a_grp[j][:].bitcast(F32)
            bank = psum.tile([P, 512], F32, name="at", tag="at", bufs=4)

            def one(s):
                lo = 512 * (r % 4) + 128 * s
                nc.tensor.transpose(out=bank[:, 128 * s:128 * (s + 1)], in_=words[:, lo:lo + 128], identity=ident[:])
                if s == 3:
                    nc.scalar.copy(
                        out=grp_words[:, 512 * t:512 * (t + 1)].rearrange("p (c i u) -> p c i u", c=2, i=128, u=2),
                        in_=bank[:].rearrange("p (c u i) -> p c i u", c=2, u=2, i=128),
                    )

            return [(one, s) for s in range(4)]

        def h_steps(j):
            g, r0, n = rounds[j]
            h_words = h_raw[g][:].bitcast(F32)
            bank = psum.tile([P, 512], F32, name="ht", tag="ht", bufs=1)
            hT[j] = work.tile([P, 512], F32, name="hT", tag="hT")

            def one(t):
                lo = 128 * (r0 + t)
                nc.tensor.transpose(out=bank[:, 128 * t:128 * (t + 1)], in_=h_words[:, lo:lo + 128], identity=ident[:])
                if t == n - 1:
                    nc.scalar.copy(out=hT[j][:, 0:128 * n], in_=bank[:, 0:128 * n])

            return [(one, t) for t in range(n)]

        def run(steps):
            for fn, arg in steps:
                fn(arg)

        def new_group(j):
            a_grp[j] = work.tile([P, 4096], BF16, name="a_grp", tag="a_grp", align_bytes=64)

        def quantise_a(k):
            a_cod[k] = work.tile([P, 1024], U32, name="a_cod", tag="a_cod", align_bytes=64)
            a_scl[k] = work.tile([P, 1024], U8, name="a_scl", tag="a_scl", align_bytes=64)
            n = rounds[k][2]
            nc.vector.quantize_mx(
                out=a_cod[k][:, 0:256 * n].bitcast(FP8X4), scales=a_scl[k][:, 0:256 * n], in_=a_grp[k][:, 0:1024 * n]
            )

        def regroup_msg(g, c):
            m_grp[g, c] = work.tile([P, 1024], BF16, name="m_grp%d" % c, tag="m_grp%d" % c, bufs=1, align_bytes=64)
            if g < V_GRAPHS:
                nc.vector.tensor_copy(
                    out=m_grp[g, c][:].rearrange("p (n i t) -> p n t i", n=64, i=4, t=4),
                    in_=m_raw[g][:, 1024 * c:1024 * (c + 1)].rearrange("p (t n i) -> p n t i", t=4, n=64, i=4),
                )
            else:
                src = m_raw[g][:, 1024 * c:1024 * (c + 1)].rearrange("p (t n) -> p n t", t=4)
                dst = m_grp[g, c][:].rearrange("p (n t) -> p n t", t=4)
                nc.gpsimd.tensor_scalar(out=dst, in0=src, scalar1=1.0, scalar2=0.0, op0=MULT, op1=ADD)

        def quantise_msg(g, c):
            m_cod[g, c] = work.tile([P, 256], U32, name="m_cod%d" % c, tag="m_cod%d" % c, align_bytes=64)
            m_scl[g, c] = work.tile([P, 256], U8, name="m_scl%d" % c, tag="m_scl%d" % c, align_bytes=64)
            nc.vector.quantize_mx(out=m_cod[g, c][:].bitcast(FP8X4), scales=m_scl[g, c][:], in_=m_grp[g, c][:])

        def self_term(k, woven):
            y[k] = work.tile([P, 1024], F32, name="y", tag="y", bufs=12)
            hT_bf = hT[k][:].bitcast(BF16)
            m = 0
            for pair in range(rounds[k][2] // 2):
                bank = psum.tile([P, 512], F32, name="acc", tag="acc", bufs=3)
                for tt in range(2):
                    t = 2 * pair + tt
                    for e in range(2):
                        run(woven[m:m + 1])
                        m += 1
                        nc.tensor.matmul(
                            out=bank[:, 256 * tt:256 * (tt + 1)],
                            lhsT=hT_bf[:, 256 * t + e:256 * (t + 1):2],
                            rhs=wsT[:, 256 * e:256 * (e + 1)],
                            start=(e == 0),
                            stop=(e == 1),
                        )
                nc.vector.tensor_tensor(out=y[k][:, 512 * pair:512 * (pair + 1)], in0=bank[:], in1=bias2[:], op=ADD)

        def aggregate(k):
            g = rounds[k][0]
            for pair in range(rounds[k][2] // 2):
                bank = psum.tile([P, 512], F32, name="acc", tag="acc", bufs=3)
                for tt in range(2):
                    t = 2 * pair + tt
                    for c in range(2):
                        lo = 256 * t + 128 * c
                        nc.tensor.matmul_mx(
                            out=bank[:, 256 * tt:256 * (tt + 1)],
                            lhsT=a_cod[k][:, lo:lo + 128].bitcast(FP8X4),
                            lhsT_scale=a_scl[k][:, lo:lo + 128],
                            rhs=m_cod[g, c][:].bitcast(FP8X4),
                            rhs_scale=m_scl[g, c][:],
                            start=(c == 0),
                            stop=(c == 1),
                        )
                half = y[k][:, 512 * pair:512 * (pair + 1)]
                nc.vector.tensor_tensor(out=half, in0=bank[:], in1=half, op=ADD)

        def relu(k):
            g, r0, n = rounds[k]
            for pair in range(n // 2):
                half = y[k][:, 512 * pair:512 * (pair + 1)]
                nc.scalar.activation(out=half, in_=half, func=RELU)
                if k == NR - 1:
                    lo = 256 * r0 + 512 * pair
                    nc.sync.dma_start(out=o_view[g][:, lo:lo + 512], in_=half)

        def store(k):
            g, r0, n = rounds[k]
            nc.sync.dma_start(out=o_view[g][:, 256 * r0:256 * (r0 + n)], in_=y[k][:, 0:256 * n])

        ident = const.tile([P, P], F32, name="ident")
        make_identity(nc, ident[:])
        w_raw = const.tile([P, 512], BF16, name="w_raw")
        nc.scalar.dma_start(out=w_raw[:].rearrange("p (o c) -> p o c", o=2), in_=Ws.rearrange("(o p) c -> p o c", p=P))
        b_row = const.tile([P, 256], BF16, name="b_row")
        nc.vector.memset(b_row[:], 0.0)
        nc.scalar.dma_start(out=b_row[0:1, :], in_=b.unsqueeze(0))
        ones = const.tile([P, P], BF16, name="ones")
        nc.vector.memset(ones[:], 1.0)

        for g in range(AHEAD + 1):
            load_graph(g)

        wsT = const.tile([P, 512], BF16, name="wsT")
        bias2 = const.tile([P, 512], F32, name="bias2")
        w_words = w_raw[:].bitcast(F32)
        w_bank = psum.tile([P, 512], F32, name="ht", tag="ht", bufs=1)
        for o in range(2):
            nc.tensor.transpose(out=w_bank[:, 128 * o:128 * (o + 1)], in_=w_words[:, 128 * o:128 * (o + 1)], identity=ident[:])
        nc.vector.tensor_copy(
            out=wsT[:].rearrange("p (e o) -> p e o", e=2),
            in_=w_bank[:, 0:256].bitcast(BF16).rearrange("p (o e) -> p e o", e=2),
        )
        b_bank = psum.tile([P, 512], F32, name="acc", tag="acc", bufs=3)
        nc.tensor.matmul(out=b_bank[:, 0:256], lhsT=ones[:], rhs=b_row[:], start=True, stop=True)
        for r in range(2):
            nc.vector.tensor_copy(out=bias2[:, 256 * r:256 * (r + 1)], in_=b_bank[:, 0:256])

        def stores_by(j):
            lag = ST_LAG if j <= rounds.index((G - 1 - AHEAD, 0, 4)) else 2
            return max(0, min(j - lag + 1, NR - 1))

        for j in range(NR + 2):
            k = j - 1
            if 1 <= j < NR and rounds[j][1] == 0 and rounds[j][0] + AHEAD < G:
                load_graph(rounds[j][0] + AHEAD)
            if j >= 2:
                relu(j - 2)
            for kk in range(stores_by(j - 1), stores_by(j)):
                store(kk)
            woven = []
            if j < NR:
                new_group(j)
                steps = []
                for t in range(rounds[j][2]):
                    steps.extend(a_tile_steps(j, t))
                steps.extend(h_steps(j))
                w = min(2 * rounds[k][2], 4 + rounds[j][2]) if (WEAVE and j >= 2) else 0
                run(steps[:len(steps) - w])
                woven = steps[len(steps) - w:]
            if j == 0:
                quantise_a(0)
                regroup_msg(0, 0)
                regroup_msg(0, 1)
                quantise_msg(0, 0)
                quantise_msg(0, 1)
                self_term(0, [])
                aggregate(0)
            if 2 <= j <= NR:
                g, r0, n = rounds[k]
                quantise_a(k)
                if r0 + n == 8 and g + 1 < G:
                    if g + 1 < V_GRAPHS:
                        regroup_msg(g + 1, 0)
                        regroup_msg(g + 1, 1)
                    quantise_msg(g + 1, 0)
                    if V_GRAPHS <= g + 2 < G:
                        regroup_msg(g + 2, 0)
                if r0 == 0 and g >= 1:
                    quantise_msg(g, 1)
                    if V_GRAPHS <= g + 1 < G:
                        regroup_msg(g + 1, 1)
                self_term(k, woven)
                aggregate(k)
